import numpy as np
import ml_dtypes


def mxq(x, axis, fmt="e4m3"):
    dtype, down = {"e4m3": (ml_dtypes.float8_e4m3fn, 7), "e5m2": (ml_dtypes.float8_e5m2, 14)}[fmt]
    v = np.moveaxis(np.asarray(x, np.float32).astype(ml_dtypes.bfloat16).astype(np.float64), axis, -1)
    blocks = v.reshape(v.shape[:-1] + (-1, 32))
    amax = np.abs(blocks).max(-1, keepdims=True)
    byte = np.maximum(np.where(amax > 0, np.frexp(amax)[1] - 1 + 127, 0) - down, 1)
    scale = np.exp2(byte - 127.0)
    codes = (blocks / scale).astype(np.float32).astype(dtype).astype(np.float64)
    return np.moveaxis((codes * scale).reshape(v.shape), -1, axis)


WIDE = False


def mx_kscale(k):
    if not WIDE:
        return np.ones(k)
    levels = np.array([10, -10, 5, -5, 0])
    a = np.random.permutation(np.resize(levels, k // 512 * 4)).reshape(k // 512, 4)
    idx = np.arange(k)
    return np.exp2(a[idx // 512, idx % 128 // 32])


BF16 = ml_dtypes.bfloat16


def bf(x):
    return np.asarray(x, np.float32).astype(BF16)


def f64(x):
    return np.asarray(x).astype(np.float64)


E2M1 = np.array([0.0, 0.5, 1.0, 1.5, 2.0, 3.0, 4.0, 6.0, -0.0, -0.5, -1.0, -1.5, -2.0, -3.0, -4.0, -6.0])


def pack_weight(w, fmt):
    k, n = w.shape
    w = f64(bf(w)).reshape(k // 32, 32, n)
    amax = np.abs(w).max(1)
    if fmt == "e4m3":
        byte = np.frexp(amax)[1] - 1 + 127 - 7
    else:
        mant, ex = np.frexp(amax / 6.0)
        byte = np.where(mant > 0.5, ex, ex - 1) + 127
    byte = np.clip(np.where(amax > 0, byte, 1), 1, 254)
    scaled = (w * np.exp2(127.0 - byte)[:, None, :]).reshape(k, n).astype(np.float32)
    by_word = np.ascontiguousarray(scaled.reshape(k // 512, 128, 4, n).transpose(0, 1, 3, 2))
    if fmt == "e4m3":
        words = by_word.astype(ml_dtypes.float8_e4m3fn).view(np.uint8)
    else:
        c = by_word.astype(ml_dtypes.float4_e2m1fn).view(np.uint8) & 0xF
        words = c[..., 0::2] | (c[..., 1::2] << 4)
    return np.ascontiguousarray(words), np.ascontiguousarray(byte.astype(np.uint8).reshape(k // 512, 16, n))


def unpack_weight(words, scales, fmt):
    g, p, n, _ = words.shape
    if fmt == "e4m3":
        vals = np.ascontiguousarray(words).view(ml_dtypes.float8_e4m3fn).astype(np.float64)
    else:
        nib = np.empty((g, p, n, 4), np.uint8)
        nib[..., 0::2] = words & 0xF
        nib[..., 1::2] = words >> 4
        vals = E2M1[nib]
    vals = vals * np.repeat(np.exp2(scales.astype(np.float64) - 127.0), 8, axis=1)[..., None]
    return vals.transpose(0, 1, 3, 2).reshape(g * 512, n)


B, S, D, H, KV, DH, W, KB = 1, 128, 8192, 16, 4, 128, 128, 512
THETA = 10000.0
FMT = "e4m3"


def rotate_half(t):
    half = t.shape[-1] // 2
    return np.concatenate((-t[..., half:], t[..., :half]), axis=-1)


def rope_cos_sin():
    inv_freq = 1.0 / THETA ** (np.arange(0, DH, 2) / DH)
    ang = np.arange(S)[:, None] * inv_freq[None, :]
    cos = np.repeat(np.cos(ang), 2, axis=-1)[None, :, None, :]
    sin = np.repeat(np.sin(ang), 2, axis=-1)[None, :, None, :]
    return cos, sin


def setup_inputs():
    s = mx_kscale(D)
    x = bf(np.random.standard_normal((B, S, D)) * s)
    Wq_words, Wq_scales = pack_weight(np.random.standard_normal((D, H * DH)) / np.sqrt(D) / s[:, None], FMT)
    Wk_words, Wk_scales = pack_weight(np.random.standard_normal((D, KV * DH)) / np.sqrt(D) / s[:, None], FMT)
    Wv_words, Wv_scales = pack_weight(np.random.standard_normal((D, KV * DH)) * 1.5 / np.sqrt(D) / s[:, None], FMT)
    return {"x": x,
            "Wq_words": Wq_words, "Wq_scales": Wq_scales,
            "Wk_words": Wk_words, "Wk_scales": Wk_scales,
            "Wv_words": Wv_words, "Wv_scales": Wv_scales}


def reference(x, Wq_words, Wq_scales, Wk_words, Wk_scales, Wv_words, Wv_scales):
    cos, sin = rope_cos_sin()
    xq = mxq(f64(x), 2, "e4m3")
    q = (xq @ unpack_weight(Wq_words, Wq_scales, FMT)).reshape(B, S, H, DH)
    k = (xq @ unpack_weight(Wk_words, Wk_scales, FMT)).reshape(B, S, KV, DH)
    v = (xq @ unpack_weight(Wv_words, Wv_scales, FMT)).reshape(B, S, KV, DH)
    q = q * cos + rotate_half(q) * sin
    k = k * cos + rotate_half(k) * sin
    return q.transpose(0, 2, 1, 3), k.transpose(0, 2, 1, 3), v.transpose(0, 2, 1, 3)

@@ -1,0 +1,261 @@
+import math
+from contextlib import ExitStack
+
+import concourse.mybir as mybir
+from concourse.masks import make_identity
+
+BF16 = mybir.dt.bfloat16
+F32 = mybir.dt.float32
+I32 = mybir.dt.int32
+U32 = mybir.dt.uint32
+U8 = mybir.dt.uint8
+FP8X4 = mybir.dt.float8_e4m3fn_x4
+ALU = mybir.AluOpType
+ACT = mybir.ActivationFunctionType
+
+P = 128
+D = 8192
+PACK = 4
+K_PASS = P * PACK
+GROUPS = D // K_PASS
+DH = 128
+HALF = DH // 2
+BANK = 512
+HEADS_PER_BANK = BANK // DH
+Q_BANKS = 4
+THETA = 10000.0
+DOUBLINGS = 6
+
+FLOPS = 2 * P * D * (16 + 4 + 4) * DH
+
+X_CHUNKS = 4
+GROUPS_PER_CHUNK = GROUPS // X_CHUNKS
+QUADRANTS = 4
+ROWS = 4
+PLANES = 4
+K_OFFSET = 0
+V_OFFSET = 4
+
+WEIGHT_WORDS = 2048
+KV_GROUPS_PER_LOAD = WEIGHT_WORDS // BANK
+WEIGHT_BUFS = 18
+
+ROUND_MAGIC = 12582912.0
+PI_HI = 3.140625
+PI_MID = round((math.pi - PI_HI) * 2.0**27) / 2.0**27
+PI_LO = math.pi - PI_HI - PI_MID
+
+
+def as_int32_rows(words):
+    return words.rearrange("p n t -> p (n t)").bitcast(I32)
+
+
+def load_x(nc, pool, x):
+    x_rows = x.rearrange("o s d -> (o s) d")
+    chunk_cols = GROUPS_PER_CHUNK * K_PASS
+    chunks = []
+    for c in range(X_CHUNKS):
+        x_chunk = pool.tile([P, chunk_cols], BF16, name="x_chunk")
+        nc.sync.dma_start(out=x_chunk[:], in_=x_rows[:, c * chunk_cols : (c + 1) * chunk_cols])
+        chunks.append(x_chunk)
+    return chunks
+
+
+def load_q_scales(nc, q_planes, Wq_scales):
+    for j in range(GROUPS // PLANES):
+        for quad in range(QUADRANTS):
+            nc.sync.dma_start(
+                out=q_planes[32 * quad : 32 * quad + PLANES * ROWS, j, :].bitcast(I32),
+                in_=Wq_scales[PLANES * j : PLANES * (j + 1), ROWS * quad : ROWS * (quad + 1), :].bitcast(I32),
+            )
+
+
+def load_kv_scales(nc, kv_planes, scales, offset):
+    for quad in range(QUADRANTS):
+        first = 32 * quad + offset
+        nc.sync.dma_start(
+            out=kv_planes[first : first + ROWS, :, :].bitcast(I32),
+            in_=scales[:, ROWS * quad : ROWS * (quad + 1), :].rearrange("g r n -> r g n").bitcast(I32),
+        )
+
+
+def quantise_x(nc, stage, psum_t, ident, x_chunks, x_codes, x_scales):
+    words_per_group = K_PASS // 2
+    groups_per_bank = 2
+    for c in range(X_CHUNKS):
+        x_words = x_chunks[c][:].bitcast(F32)
+        grouped = stage.tile([P, GROUPS_PER_CHUNK, P, PACK], BF16, align_bytes=64)
+        for b in range(GROUPS_PER_CHUNK // groups_per_bank):
+            xt = psum_t.tile([P, groups_per_bank, 2, P], F32)
+            for gb in range(groups_per_bank):
+                first_word = (b * groups_per_bank + gb) * words_per_group
+                for u in range(2):
+                    nc.tensor.transpose(
+                        xt[:, gb, u, :],
+                        x_words[:, first_word + u : first_word + words_per_group : 2],
+                        ident[:],
+                    )
+            out_words = grouped[:, b * groups_per_bank : (b + 1) * groups_per_bank, :, :].bitcast(F32)
+            in_words = xt[:].rearrange("p g u r -> p g r u")
+            if b % 2 == 0:
+                nc.vector.tensor_copy(out=out_words, in_=in_words)
+            else:
+                nc.scalar.copy(out=out_words, in_=in_words)
+        groups = slice(c * GROUPS_PER_CHUNK, (c + 1) * GROUPS_PER_CHUNK)
+        nc.vector.quantize_mx(
+            out=x_codes[:, groups, :].rearrange("p g r -> p (g r)").bitcast(FP8X4),
+            scales=x_scales[:, groups, :].rearrange("p g r -> p (g r)"),
+            in_=grouped[:].rearrange("p g r t -> p (g r t)"),
+        )
+
+
+def rope_tables(nc, const):
+    position = const.tile([P, 2], F32)
+    nc.gpsimd.iota(
+        position[:], pattern=[[0, 2]], base=0, channel_multiplier=1, allow_small_or_imprecise_dtypes=True
+    )
+    half_angle = const.tile([P, DH], F32)
+    nc.vector.tensor_scalar(out=half_angle[:, 0:2], in0=position[:], scalar1=0.5, scalar2=None, op0=ALU.mult)
+    for doubling in range(DOUBLINGS):
+        width = 2 * 2**doubling
+        nc.vector.tensor_scalar(
+            out=half_angle[:, width : 2 * width],
+            in0=half_angle[:, 0:width],
+            scalar1=THETA ** (-width / DH),
+            scalar2=None,
+            op0=ALU.mult,
+        )
+
+    turns = const.tile([P, DH], F32)
+    nc.vector.tensor_scalar(
+        out=turns[:], in0=half_angle[:], scalar1=1.0 / math.pi, scalar2=ROUND_MAGIC, op0=ALU.mult, op1=ALU.add
+    )
+    nc.vector.tensor_scalar(out=turns[:], in0=turns[:], scalar1=ROUND_MAGIC, scalar2=None, op0=ALU.subtract)
+    reduced = const.tile([P, DH], F32)
+    nc.vector.scalar_tensor_tensor(
+        out=reduced[:], in0=turns[:], scalar=-PI_HI, in1=half_angle[:], op0=ALU.mult, op1=ALU.add
+    )
+    for piece in (PI_MID, PI_LO):
+        nc.vector.scalar_tensor_tensor(
+            out=reduced[:], in0=turns[:], scalar=-piece, in1=reduced[:], op0=ALU.mult, op1=ALU.add
+        )
+
+    sin_h = const.tile([P, DH], F32)
+    nc.scalar.activation(out=sin_h[:], in_=reduced[:], func=ACT.Sin)
+    sin_h2 = const.tile([P, DH], F32)
+    nc.scalar.activation(out=sin_h2[:], in_=reduced[:], func=ACT.Sin, scale=0.5)
+
+    cos_h = const.tile([P, DH], F32)
+    nc.vector.tensor_mul(out=cos_h[:], in0=sin_h2[:], in1=sin_h2[:])
+    nc.vector.tensor_scalar(out=cos_h[:], in0=cos_h[:], scalar1=-2.0, scalar2=1.0, op0=ALU.mult, op1=ALU.add)
+    cos_a = const.tile([P, DH], F32)
+    nc.vector.tensor_mul(out=cos_a[:], in0=sin_h[:], in1=sin_h[:])
+    nc.vector.tensor_scalar(out=cos_a[:], in0=cos_a[:], scalar1=-2.0, scalar2=1.0, op0=ALU.mult, op1=ALU.add)
+    sin_a = const.tile([P, DH], F32)
+    for cols, sign in ((slice(0, HALF), -1.0), (slice(HALF, DH), 1.0)):
+        nc.vector.scalar_tensor_tensor(
+            out=sin_a[:, cols], in0=sin_h[:, cols], scalar=2.0 * sign, in1=cos_h[:, cols], op0=ALU.mult, op1=ALU.mult
+        )
+    return cos_a, sin_a
+
+
+def rotate_and_store(nc, work, acc, cos_a, sin_a, out_heads):
+    rotated = work.tile([P, HEADS_PER_BANK, DH], F32)
+    nc.vector.tensor_tensor(
+        out=rotated[:],
+        in0=acc[:].rearrange("p (h i) -> p h i", i=DH),
+        in1=cos_a[:].unsqueeze(1).to_broadcast([P, HEADS_PER_BANK, DH]),
+        op=ALU.mult,
+    )
+    halves = acc[:].rearrange("p (h s j) -> p h s j", s=2, j=HALF)
+    crossed = work.tile([P, HEADS_PER_BANK, 2, HALF], F32)
+    for s in range(2):
+        nc.vector.tensor_tensor(
+            out=crossed[:, :, s, :],
+            in0=halves[:, :, 1 - s, :],
+            in1=sin_a[:, s * HALF : (s + 1) * HALF].unsqueeze(1).to_broadcast([P, HEADS_PER_BANK, HALF]),
+            op=ALU.mult,
+        )
+    nc.vector.tensor_add(out=rotated[:], in0=rotated[:], in1=crossed[:].rearrange("p h s j -> p h (s j)"))
+    nc.gpsimd.dma_start(out=out_heads, in_=rotated[:])
+
+
+def tile_spikinggroupedslidingattention_pa_k_kernel(
+    tc, x, Wq_words, Wq_scales, Wk_words, Wk_scales, Wv_words, Wv_scales, out_0, out_1, out_2
+):
+    nc = tc.nc
+    q_out = out_0.rearrange("o h p i -> p (o h) i")
+    k_out = out_1.rearrange("o h p i -> p (o h) i")
+    v_out = out_2.rearrange("o h p i -> p (o h) i")
+
+    with ExitStack() as ctx:
+        ctx.enter_context(tc.manual_schedule())
+        const = ctx.enter_context(tc.tile_pool(name="const", bufs=1))
+        keep = ctx.enter_context(tc.tile_pool(name="keep", bufs=1))
+        x_pool = ctx.enter_context(tc.tile_pool(name="x_pool", bufs=X_CHUNKS))
+        stage = ctx.enter_context(tc.tile_pool(name="stage", bufs=2))
+        weights = ctx.enter_context(tc.tile_pool(name="weights", bufs=WEIGHT_BUFS))
+        work = ctx.enter_context(tc.tile_pool(name="work", bufs=2))
+        psum_t = ctx.enter_context(tc.psum_pool(name="psum_t", bufs=2))
+        psum_acc = ctx.enter_context(tc.psum_pool(name="psum_acc", bufs=1))
+
+        x_codes = keep.tile([P, GROUPS, P], U32, align_bytes=64)
+        x_scales = keep.tile([P, GROUPS, P], U8, align_bytes=64)
+        q_planes = keep.tile([P, GROUPS // PLANES, Q_BANKS * BANK], U8, align_bytes=64)
+        kv_planes = keep.tile([P, GROUPS, BANK], U8, align_bytes=64)
+
+        nc.vector.memset(q_planes[:].rearrange("p j n -> p (j n)").bitcast(I32), 0)
+        nc.vector.memset(kv_planes[:].rearrange("p g n -> p (g n)").bitcast(I32), 0)
+        ident = const.tile([P, P], F32)
+        make_identity(nc, ident[:])
+
+        x_chunks = load_x(nc, x_pool, x)
+        load_q_scales(nc, q_planes, Wq_scales)
+        load_kv_scales(nc, kv_planes, Wk_scales, K_OFFSET)
+        load_kv_scales(nc, kv_planes, Wv_scales, V_OFFSET)
+
+        quantise_x(nc, stage, psum_t, ident, x_chunks, x_codes, x_scales)
+        cos_a, sin_a = rope_tables(nc, const)
+
+        def multiply(acc, g, w_words, w_plane):
+            nc.tensor.matmul_mx(
+                out=acc[:],
+                lhsT=x_codes[:, g, :].bitcast(FP8X4),
+                lhsT_scale=x_scales[:, g, :],
+                rhs=w_words.bitcast(FP8X4),
+                rhs_scale=w_plane,
+                start=(g == 0),
+                stop=(g == GROUPS - 1),
+            )
+
+        acc_q = [psum_acc.tile([P, BANK], F32, name="acc_q%d" % b) for b in range(Q_BANKS)]
+        for g in range(GROUPS):
+            w = weights.tile([P, WEIGHT_WORDS], U32, align_bytes=64)
+            nc.sync.dma_start(out=w[:].bitcast(I32), in_=as_int32_rows(Wq_words[g]))
+            for b in range(Q_BANKS):
+                cols = slice(b * BANK, (b + 1) * BANK)
+                multiply(acc_q[b], g, w[:, cols], q_planes[ROWS * (g % PLANES) : P, g // PLANES, cols])
+        for b in range(Q_BANKS):
+            rotate_and_store(
+                nc, work, acc_q[b], cos_a, sin_a, q_out[:, b * HEADS_PER_BANK : (b + 1) * HEADS_PER_BANK, :]
+            )
+
+        def project_kv(acc, words, offset):
+            for first in range(0, GROUPS, KV_GROUPS_PER_LOAD):
+                w = weights.tile([P, WEIGHT_WORDS], U32, align_bytes=64)
+                nc.sync.dma_start(
+                    out=w[:].rearrange("p (g n) -> p g n", g=KV_GROUPS_PER_LOAD).bitcast(I32),
+                    in_=words[first : first + KV_GROUPS_PER_LOAD].rearrange("g p n t -> p g (n t)").bitcast(I32),
+                )
+                for i in range(KV_GROUPS_PER_LOAD):
+                    multiply(acc, first + i, w[:, i * BANK : (i + 1) * BANK], kv_planes[offset:P, first + i, :])
+
+        acc_k = psum_acc.tile([P, BANK], F32)
+        project_kv(acc_k, Wk_words, K_OFFSET)
+        rotate_and_store(nc, work, acc_k, cos_a, sin_a, k_out)
+
+        acc_v = psum_acc.tile([P, BANK], F32)
+        project_kv(acc_v, Wv_words, V_OFFSET)
+        v_heads = work.tile([P, HEADS_PER_BANK, DH], F32)
+        nc.vector.tensor_copy(out=v_heads[:].rearrange("p h i -> p (h i)"), in_=acc_v[:])
+        nc.sync.dma_start(out=v_out, in_=v_heads[:])

@@ -159,8 +159,8 @@ def rope_tables(nc, const):
     return cos_a, sin_a
 
 
-def rotate_and_store(nc, work, acc, cos_a, sin_a, out_heads):
-    rotated = work.tile([P, HEADS_PER_BANK, DH], F32)
+def rotate_and_store(nc, work, results, acc, cos_a, sin_a, out_heads):
+    rotated = results.tile([P, HEADS_PER_BANK, DH], F32)
     nc.vector.tensor_tensor(
         out=rotated[:],
         in0=acc[:].rearrange("p (h i) -> p h i", i=DH),
@@ -196,6 +196,7 @@ def tile_spikinggroupedslidingattention_pa_k_kernel(
         stage = ctx.enter_context(tc.tile_pool(name="stage", bufs=2))
         weights = ctx.enter_context(tc.tile_pool(name="weights", bufs=WEIGHT_BUFS))
         work = ctx.enter_context(tc.tile_pool(name="work", bufs=2))
+        results = ctx.enter_context(tc.tile_pool(name="results", bufs=Q_BANKS + 1))
         psum_t = ctx.enter_context(tc.psum_pool(name="psum_t", bufs=2))
         psum_acc = ctx.enter_context(tc.psum_pool(name="psum_acc", bufs=1))
 
@@ -236,9 +237,8 @@ def tile_spikinggroupedslidingattention_pa_k_kernel(
                 cols = slice(b * BANK, (b + 1) * BANK)
                 multiply(acc_q[b], g, w[:, cols], q_planes[ROWS * (g % PLANES) : P, g // PLANES, cols])
         for b in range(Q_BANKS):
-            rotate_and_store(
-                nc, work, acc_q[b], cos_a, sin_a, q_out[:, b * HEADS_PER_BANK : (b + 1) * HEADS_PER_BANK, :]
-            )
+            heads = slice(b * HEADS_PER_BANK, (b + 1) * HEADS_PER_BANK)
+            rotate_and_store(nc, work, results, acc_q[b], cos_a, sin_a, q_out[:, heads, :])
 
         def project_kv(acc, words, offset):
             for first in range(0, GROUPS, KV_GROUPS_PER_LOAD):
@@ -252,7 +252,7 @@ def tile_spikinggroupedslidingattention_pa_k_kernel(
 
         acc_k = psum_acc.tile([P, BANK], F32)
         project_kv(acc_k, Wk_words, K_OFFSET)
-        rotate_and_store(nc, work, acc_k, cos_a, sin_a, k_out)
+        rotate_and_store(nc, work, results, acc_k, cos_a, sin_a, k_out)
 
         acc_v = psum_acc.tile([P, BANK], F32)
         project_kv(acc_v, Wv_words, V_OFFSET)

@@ -64,19 +64,16 @@ def load_x(nc, pool, x):
 def load_q_scales(nc, q_planes, Wq_scales):
     for j in range(GROUPS // PLANES):
         for quad in range(QUADRANTS):
-            nc.sync.dma_start(
-                out=q_planes[32 * quad : 32 * quad + PLANES * ROWS, j, :].bitcast(I32),
-                in_=Wq_scales[PLANES * j : PLANES * (j + 1), ROWS * quad : ROWS * (quad + 1), :].bitcast(I32),
+            nc.gpsimd.dma_start(
+                out=q_planes[32 * quad : 32 * quad + PLANES * ROWS, j, :].bitcast(F32),
+                in_=Wq_scales[PLANES * j : PLANES * (j + 1), ROWS * quad : ROWS * (quad + 1), :].bitcast(F32),
             )
 
 
 def load_kv_scales(nc, kv_planes, scales, offset):
-    for quad in range(QUADRANTS):
-        first = 32 * quad + offset
-        nc.sync.dma_start(
-            out=kv_planes[first : first + ROWS, :, :].bitcast(I32),
-            in_=scales[:, ROWS * quad : ROWS * (quad + 1), :].rearrange("g r n -> r g n").bitcast(I32),
-        )
+    by_row = scales.rearrange("g (quad r) n -> r quad g n", r=ROWS)
+    for r in range(ROWS):
+        nc.gpsimd.dma_start(out=kv_planes[offset + r : P : 32, :, :].bitcast(F32), in_=by_row[r].bitcast(F32))
 
 
 def quantise_x(nc, stage, psum_t, ident, x_chunks, x_codes, x_scales):
@@ -109,11 +106,7 @@ def quantise_x(nc, stage, psum_t, ident, x_chunks, x_codes, x_scales):
         )
 
 
-def rope_tables(nc, const):
-    position = const.tile([P, 2], F32)
-    nc.gpsimd.iota(
-        position[:], pattern=[[0, 2]], base=0, channel_multiplier=1, allow_small_or_imprecise_dtypes=True
-    )
+def rope_tables(nc, const, position):
     half_angle = const.tile([P, DH], F32)
     nc.vector.tensor_scalar(out=half_angle[:, 0:2], in0=position[:], scalar1=0.5, scalar2=None, op0=ALU.mult)
     for doubling in range(DOUBLINGS):
@@ -209,6 +202,10 @@ def tile_spikinggroupedslidingattention_pa_k_kernel(
         nc.vector.memset(kv_planes[:].rearrange("p g n -> p (g n)").bitcast(I32), 0)
         ident = const.tile([P, P], F32)
         make_identity(nc, ident[:])
+        position = const.tile([P, 2], F32)
+        nc.gpsimd.iota(
+            position[:], pattern=[[0, 2]], base=0, channel_multiplier=1, allow_small_or_imprecise_dtypes=True
+        )
 
         x_chunks = load_x(nc, x_pool, x)
         load_q_scales(nc, q_planes, Wq_scales)
@@ -216,7 +213,7 @@ def tile_spikinggroupedslidingattention_pa_k_kernel(
         load_kv_scales(nc, kv_planes, Wv_scales, V_OFFSET)
 
         quantise_x(nc, stage, psum_t, ident, x_chunks, x_codes, x_scales)
-        cos_a, sin_a = rope_tables(nc, const)
+        cos_a, sin_a = rope_tables(nc, const, position)
 
         def multiply(acc, g, w_words, w_plane):
             nc.tensor.matmul_mx(

@@ -152,7 +152,7 @@ def rope_tables(nc, const, position):
     return cos_a, sin_a
 
 
-def rotate_and_store(nc, work, results, acc, cos_a, sin_a, out_heads):
+def rotate(nc, work, results, acc, cos_a, sin_a):
     rotated = results.tile([P, HEADS_PER_BANK, DH], F32)
     nc.vector.tensor_tensor(
         out=rotated[:],
@@ -170,7 +170,7 @@ def rotate_and_store(nc, work, results, acc, cos_a, sin_a, out_heads):
             op=ALU.mult,
         )
     nc.vector.tensor_add(out=rotated[:], in0=rotated[:], in1=crossed[:].rearrange("p h s j -> p h (s j)"))
-    nc.gpsimd.dma_start(out=out_heads, in_=rotated[:])
+    return rotated
 
 
 def tile_spikinggroupedslidingattention_pa_k_kernel(
@@ -233,9 +233,7 @@ def tile_spikinggroupedslidingattention_pa_k_kernel(
             for b in range(Q_BANKS):
                 cols = slice(b * BANK, (b + 1) * BANK)
                 multiply(acc_q[b], g, w[:, cols], q_planes[ROWS * (g % PLANES) : P, g // PLANES, cols])
-        for b in range(Q_BANKS):
-            heads = slice(b * HEADS_PER_BANK, (b + 1) * HEADS_PER_BANK)
-            rotate_and_store(nc, work, results, acc_q[b], cos_a, sin_a, q_out[:, heads, :])
+        q_rotated = [rotate(nc, work, results, acc_q[b], cos_a, sin_a) for b in range(Q_BANKS)]
 
         def project_kv(acc, words, offset):
             for first in range(0, GROUPS, KV_GROUPS_PER_LOAD):
@@ -249,10 +247,14 @@ def tile_spikinggroupedslidingattention_pa_k_kernel(
 
         acc_k = psum_acc.tile([P, BANK], F32)
         project_kv(acc_k, Wk_words, K_OFFSET)
-        rotate_and_store(nc, work, results, acc_k, cos_a, sin_a, k_out)
+        k_rotated = rotate(nc, work, results, acc_k, cos_a, sin_a)
 
         acc_v = psum_acc.tile([P, BANK], F32)
         project_kv(acc_v, Wv_words, V_OFFSET)
+
+        for b in range(Q_BANKS):
+            nc.sync.dma_start(out=q_out[:, b * HEADS_PER_BANK : (b + 1) * HEADS_PER_BANK, :], in_=q_rotated[b][:])
+        nc.sync.dma_start(out=k_out, in_=k_rotated[:])
         v_heads = work.tile([P, HEADS_PER_BANK, DH], F32)
         nc.vector.tensor_copy(out=v_heads[:].rearrange("p h i -> p (h i)"), in_=acc_v[:])
         nc.sync.dma_start(out=v_out, in_=v_heads[:])

@@ -238,11 +238,10 @@ def tile_spikinggroupedslidingattention_pa_k_kernel(
         def project_kv(acc, words, offset):
             for first in range(0, GROUPS, KV_GROUPS_PER_LOAD):
                 w = weights.tile([P, WEIGHT_WORDS], U32, align_bytes=64)
-                nc.sync.dma_start(
-                    out=w[:].rearrange("p (g n) -> p g n", g=KV_GROUPS_PER_LOAD).bitcast(I32),
-                    in_=words[first : first + KV_GROUPS_PER_LOAD].rearrange("g p n t -> p g (n t)").bitcast(I32),
-                )
                 for i in range(KV_GROUPS_PER_LOAD):
+                    nc.sync.dma_start(
+                        out=w[:, i * BANK : (i + 1) * BANK].bitcast(I32), in_=as_int32_rows(words[first + i])
+                    )
                     multiply(acc, first + i, w[:, i * BANK : (i + 1) * BANK], kv_planes[offset:P, first + i, :])
 
         acc_k = psum_acc.tile([P, BANK], F32)

@@ -70,10 +70,13 @@ def load_q_scales(nc, q_planes, Wq_scales):
             )
 
 
-def load_kv_scales(nc, kv_planes, scales, offset):
-    by_row = scales.rearrange("g (quad r) n -> r quad g n", r=ROWS)
-    for r in range(ROWS):
-        nc.gpsimd.dma_start(out=kv_planes[offset + r : P : 32, :, :].bitcast(F32), in_=by_row[r].bitcast(F32))
+def load_kv_scale_row(nc, kv_planes, scales, offset, row):
+    quad, r = divmod(row, ROWS)
+    partition = 32 * quad + offset + r
+    nc.sync.dma_start(
+        out=kv_planes[partition : partition + 1, :, :].bitcast(I32),
+        in_=scales[:, row : row + 1, :].rearrange("g q n -> q g n").bitcast(I32),
+    )
 
 
 def quantise_x(nc, stage, psum_t, ident, x_chunks, x_codes, x_scales):
@@ -209,8 +212,6 @@ def tile_spikinggroupedslidingattention_pa_k_kernel(
 
         x_chunks = load_x(nc, x_pool, x)
         load_q_scales(nc, q_planes, Wq_scales)
-        load_kv_scales(nc, kv_planes, Wk_scales, K_OFFSET)
-        load_kv_scales(nc, kv_planes, Wv_scales, V_OFFSET)
 
         quantise_x(nc, stage, psum_t, ident, x_chunks, x_codes, x_scales)
         cos_a, sin_a = rope_tables(nc, const, position)
@@ -230,6 +231,8 @@ def tile_spikinggroupedslidingattention_pa_k_kernel(
         for g in range(GROUPS):
             w = weights.tile([P, WEIGHT_WORDS], U32, align_bytes=64)
             nc.sync.dma_start(out=w[:].bitcast(I32), in_=as_int32_rows(Wq_words[g]))
+            load_kv_scale_row(nc, kv_planes, Wk_scales, K_OFFSET, g)
+            load_kv_scale_row(nc, kv_planes, Wv_scales, V_OFFSET, g)
             for b in range(Q_BANKS):
                 cols = slice(b * BANK, (b + 1) * BANK)
                 multiply(acc_q[b], g, w[:, cols], q_planes[ROWS * (g % PLANES) : P, g // PLANES, cols])

@@ -33,8 +33,6 @@ GROUPS_PER_CHUNK = GROUPS // X_CHUNKS
 QUADRANTS = 4
 ROWS = 4
 PLANES = 4
-K_OFFSET = 0
-V_OFFSET = 4
 
 WEIGHT_WORDS = 2048
 KV_GROUPS_PER_LOAD = WEIGHT_WORDS // BANK
@@ -61,21 +59,10 @@ def load_x(nc, pool, x):
     return chunks
 
 
-def load_q_scales(nc, q_planes, Wq_scales):
-    for j in range(GROUPS // PLANES):
-        for quad in range(QUADRANTS):
-            nc.gpsimd.dma_start(
-                out=q_planes[32 * quad : 32 * quad + PLANES * ROWS, j, :].bitcast(F32),
-                in_=Wq_scales[PLANES * j : PLANES * (j + 1), ROWS * quad : ROWS * (quad + 1), :].bitcast(F32),
-            )
-
-
-def load_kv_scale_row(nc, kv_planes, scales, offset, row):
-    quad, r = divmod(row, ROWS)
-    partition = 32 * quad + offset + r
-    nc.sync.dma_start(
-        out=kv_planes[partition : partition + 1, :, :].bitcast(I32),
-        in_=scales[:, row : row + 1, :].rearrange("g q n -> q g n").bitcast(I32),
+def load_scale_block(queue, word, planes, scales, j, quad):
+    queue.dma_start(
+        out=planes[32 * quad : 32 * quad + PLANES * ROWS, j, :].bitcast(word),
+        in_=scales[PLANES * j : PLANES * (j + 1), ROWS * quad : ROWS * (quad + 1), :].bitcast(word),
     )
 
 
@@ -199,10 +186,11 @@ def tile_spikinggroupedslidingattention_pa_k_kernel(
         x_codes = keep.tile([P, GROUPS, P], U32, align_bytes=64)
         x_scales = keep.tile([P, GROUPS, P], U8, align_bytes=64)
         q_planes = keep.tile([P, GROUPS // PLANES, Q_BANKS * BANK], U8, align_bytes=64)
-        kv_planes = keep.tile([P, GROUPS, BANK], U8, align_bytes=64)
+        k_planes = keep.tile([P, GROUPS // PLANES, BANK], U8, align_bytes=64)
+        v_planes = keep.tile([P, GROUPS // PLANES, BANK], U8, align_bytes=64)
 
-        nc.vector.memset(q_planes[:].rearrange("p j n -> p (j n)").bitcast(I32), 0)
-        nc.vector.memset(kv_planes[:].rearrange("p g n -> p (g n)").bitcast(I32), 0)
+        for planes in (q_planes, k_planes, v_planes):
+            nc.vector.memset(planes[:].rearrange("p j n -> p (j n)").bitcast(I32), 0)
         ident = const.tile([P, P], F32)
         make_identity(nc, ident[:])
         position = const.tile([P, 2], F32)
@@ -211,7 +199,10 @@ def tile_spikinggroupedslidingattention_pa_k_kernel(
         )
 
         x_chunks = load_x(nc, x_pool, x)
-        load_q_scales(nc, q_planes, Wq_scales)
+        blocks = [(j, quad) for j in range(GROUPS // PLANES) for quad in range(QUADRANTS)]
+        for planes, scales in ((q_planes, Wq_scales), (v_planes, Wv_scales)):
+            for j, quad in blocks:
+                load_scale_block(nc.gpsimd, F32, planes, scales, j, quad)
 
         quantise_x(nc, stage, psum_t, ident, x_chunks, x_codes, x_scales)
         cos_a, sin_a = rope_tables(nc, const, position)
@@ -231,28 +222,28 @@ def tile_spikinggroupedslidingattention_pa_k_kernel(
         for g in range(GROUPS):
             w = weights.tile([P, WEIGHT_WORDS], U32, align_bytes=64)
             nc.sync.dma_start(out=w[:].bitcast(I32), in_=as_int32_rows(Wq_words[g]))
-            load_kv_scale_row(nc, kv_planes, Wk_scales, K_OFFSET, g)
-            load_kv_scale_row(nc, kv_planes, Wv_scales, V_OFFSET, g)
+            load_scale_block(nc.sync, I32, k_planes, Wk_scales, *blocks[g])
             for b in range(Q_BANKS):
                 cols = slice(b * BANK, (b + 1) * BANK)
                 multiply(acc_q[b], g, w[:, cols], q_planes[ROWS * (g % PLANES) : P, g // PLANES, cols])
         q_rotated = [rotate(nc, work, results, acc_q[b], cos_a, sin_a) for b in range(Q_BANKS)]
 
-        def project_kv(acc, words, offset):
+        def project_kv(acc, words, planes):
             for first in range(0, GROUPS, KV_GROUPS_PER_LOAD):
                 w = weights.tile([P, WEIGHT_WORDS], U32, align_bytes=64)
                 for i in range(KV_GROUPS_PER_LOAD):
                     nc.sync.dma_start(
                         out=w[:, i * BANK : (i + 1) * BANK].bitcast(I32), in_=as_int32_rows(words[first + i])
                     )
-                    multiply(acc, first + i, w[:, i * BANK : (i + 1) * BANK], kv_planes[offset:P, first + i, :])
+                    j, c = divmod(first + i, PLANES)
+                    multiply(acc, first + i, w[:, i * BANK : (i + 1) * BANK], planes[ROWS * c : P, j, :])
 
         acc_k = psum_acc.tile([P, BANK], F32)
-        project_kv(acc_k, Wk_words, K_OFFSET)
+        project_kv(acc_k, Wk_words, k_planes)
         k_rotated = rotate(nc, work, results, acc_k, cos_a, sin_a)
 
         acc_v = psum_acc.tile([P, BANK], F32)
-        project_kv(acc_v, Wv_words, V_OFFSET)
+        project_kv(acc_v, Wv_words, v_planes)
 
         for b in range(Q_BANKS):
             nc.sync.dma_start(out=q_out[:, b * HEADS_PER_BANK : (b + 1) * HEADS_PER_BANK, :], in_=q_rotated[b][:])

@@ -29,14 +29,19 @@ DOUBLINGS = 6
 FLOPS = 2 * P * D * (16 + 4 + 4) * DH
 
 X_CHUNKS = 4
+X_LOADS = 2
+CHUNKS_PER_LOAD = X_CHUNKS // X_LOADS
 GROUPS_PER_CHUNK = GROUPS // X_CHUNKS
 QUADRANTS = 4
 ROWS = 4
 PLANES = 4
 
-WEIGHT_WORDS = 2048
-KV_GROUPS_PER_LOAD = WEIGHT_WORDS // BANK
-WEIGHT_BUFS = 18
+WEIGHT_WORDS = 4096
+Q_GROUPS_PER_TILE = 2
+KV_GROUPS_PER_TILE = WEIGHT_WORDS // BANK
+WEIGHT_BUFS = 9
+K_LOADS = (8, 8)
+V_LOADS = (8, 4, 3, 1)
 
 ROUND_MAGIC = 12582912.0
 PI_HI = 3.140625
@@ -44,18 +49,22 @@ PI_MID = round((math.pi - PI_HI) * 2.0**27) / 2.0**27
 PI_LO = math.pi - PI_HI - PI_MID
 
 
-def as_int32_rows(words):
-    return words.rearrange("p n t -> p (n t)").bitcast(I32)
+def load_groups(nc, w, words, first, count, width, slot):
+    nc.sync.dma_start(
+        out=w[:, slot * width : (slot + count) * width].rearrange("p (g n) -> p g n", g=count).bitcast(I32),
+        in_=words[first : first + count].rearrange("g p n t -> p g (n t)").bitcast(I32),
+    )
 
 
 def load_x(nc, pool, x):
     x_rows = x.rearrange("o s d -> (o s) d")
     chunk_cols = GROUPS_PER_CHUNK * K_PASS
+    load_cols = CHUNKS_PER_LOAD * chunk_cols
     chunks = []
-    for c in range(X_CHUNKS):
-        x_chunk = pool.tile([P, chunk_cols], BF16, name="x_chunk")
-        nc.sync.dma_start(out=x_chunk[:], in_=x_rows[:, c * chunk_cols : (c + 1) * chunk_cols])
-        chunks.append(x_chunk)
+    for load in range(X_LOADS):
+        x_part = pool.tile([P, load_cols], BF16, name="x_part")
+        nc.sync.dma_start(out=x_part[:], in_=x_rows[:, load * load_cols : (load + 1) * load_cols])
+        chunks += [x_part[:, c * chunk_cols : (c + 1) * chunk_cols] for c in range(CHUNKS_PER_LOAD)]
     return chunks
 
 
@@ -70,7 +79,7 @@ def quantise_x(nc, stage, psum_t, ident, x_chunks, x_codes, x_scales):
     words_per_group = K_PASS // 2
     groups_per_bank = 2
     for c in range(X_CHUNKS):
-        x_words = x_chunks[c][:].bitcast(F32)
+        x_words = x_chunks[c].bitcast(F32)
         grouped = stage.tile([P, GROUPS_PER_CHUNK, P, PACK], BF16, align_bytes=64)
         for b in range(GROUPS_PER_CHUNK // groups_per_bank):
             xt = psum_t.tile([P, groups_per_bank, 2, P], F32)
@@ -175,7 +184,7 @@ def tile_spikinggroupedslidingattention_pa_k_kernel(
         ctx.enter_context(tc.manual_schedule())
         const = ctx.enter_context(tc.tile_pool(name="const", bufs=1))
         keep = ctx.enter_context(tc.tile_pool(name="keep", bufs=1))
-        x_pool = ctx.enter_context(tc.tile_pool(name="x_pool", bufs=X_CHUNKS))
+        x_pool = ctx.enter_context(tc.tile_pool(name="x_pool", bufs=X_LOADS))
         stage = ctx.enter_context(tc.tile_pool(name="stage", bufs=2))
         weights = ctx.enter_context(tc.tile_pool(name="weights", bufs=WEIGHT_BUFS))
         work = ctx.enter_context(tc.tile_pool(name="work", bufs=2))
@@ -219,31 +228,36 @@ def tile_spikinggroupedslidingattention_pa_k_kernel(
             )
 
         acc_q = [psum_acc.tile([P, BANK], F32, name="acc_q%d" % b) for b in range(Q_BANKS)]
-        for g in range(GROUPS):
+        for first in range(0, GROUPS, Q_GROUPS_PER_TILE):
             w = weights.tile([P, WEIGHT_WORDS], U32, align_bytes=64)
-            nc.sync.dma_start(out=w[:].bitcast(I32), in_=as_int32_rows(Wq_words[g]))
-            load_scale_block(nc.sync, I32, k_planes, Wk_scales, *blocks[g])
-            for b in range(Q_BANKS):
-                cols = slice(b * BANK, (b + 1) * BANK)
-                multiply(acc_q[b], g, w[:, cols], q_planes[ROWS * (g % PLANES) : P, g // PLANES, cols])
+            load_groups(nc, w, Wq_words, first, Q_GROUPS_PER_TILE, Q_BANKS * BANK, 0)
+            for i in range(Q_GROUPS_PER_TILE):
+                g = first + i
+                load_scale_block(nc.sync, I32, k_planes, Wk_scales, *blocks[g])
+                for b in range(Q_BANKS):
+                    word = (i * Q_BANKS + b) * BANK
+                    q_plane = q_planes[ROWS * (g % PLANES) : P, g // PLANES, b * BANK : (b + 1) * BANK]
+                    multiply(acc_q[b], g, w[:, word : word + BANK], q_plane)
         q_rotated = [rotate(nc, work, results, acc_q[b], cos_a, sin_a) for b in range(Q_BANKS)]
 
-        def project_kv(acc, words, planes):
-            for first in range(0, GROUPS, KV_GROUPS_PER_LOAD):
-                w = weights.tile([P, WEIGHT_WORDS], U32, align_bytes=64)
-                for i in range(KV_GROUPS_PER_LOAD):
-                    nc.sync.dma_start(
-                        out=w[:, i * BANK : (i + 1) * BANK].bitcast(I32), in_=as_int32_rows(words[first + i])
-                    )
-                    j, c = divmod(first + i, PLANES)
-                    multiply(acc, first + i, w[:, i * BANK : (i + 1) * BANK], planes[ROWS * c : P, j, :])
+        def project_kv(acc, words, planes, loads):
+            g = 0
+            for count in loads:
+                slot = g % KV_GROUPS_PER_TILE
+                if slot == 0:
+                    w = weights.tile([P, WEIGHT_WORDS], U32, align_bytes=64)
+                load_groups(nc, w, words, g, count, BANK, slot)
+                for i in range(slot, slot + count):
+                    j, c = divmod(g, PLANES)
+                    multiply(acc, g, w[:, i * BANK : (i + 1) * BANK], planes[ROWS * c : P, j, :])
+                    g += 1
 
         acc_k = psum_acc.tile([P, BANK], F32)
-        project_kv(acc_k, Wk_words, k_planes)
+        project_kv(acc_k, Wk_words, k_planes, K_LOADS)
         k_rotated = rotate(nc, work, results, acc_k, cos_a, sin_a)
 
         acc_v = psum_acc.tile([P, BANK], F32)
-        project_kv(acc_v, Wv_words, v_planes)
+        project_kv(acc_v, Wv_words, v_planes, V_LOADS)
 
         for b in range(Q_BANKS):
             nc.sync.dma_start(out=q_out[:, b * HEADS_PER_BANK : (b + 1) * HEADS_PER_BANK, :], in_=q_rotated[b][:])

import math
from contextlib import ExitStack

import concourse.mybir as mybir
from concourse.masks import make_identity

BF16 = mybir.dt.bfloat16
F32 = mybir.dt.float32
I32 = mybir.dt.int32
U32 = mybir.dt.uint32
U8 = mybir.dt.uint8
FP8X4 = mybir.dt.float8_e4m3fn_x4
ALU = mybir.AluOpType
ACT = mybir.ActivationFunctionType

P = 128
D = 8192
PACK = 4
K_PASS = P * PACK
GROUPS = D // K_PASS
DH = 128
HALF = DH // 2
BANK = 512
HEADS_PER_BANK = BANK // DH
Q_BANKS = 4
THETA = 10000.0
DOUBLINGS = 6

FLOPS = 2 * P * D * (16 + 4 + 4) * DH

X_CHUNKS = 4
X_LOADS = 2
CHUNKS_PER_LOAD = X_CHUNKS // X_LOADS
GROUPS_PER_CHUNK = GROUPS // X_CHUNKS
QUADRANTS = 4
ROWS = 4
PLANES = 4

WEIGHT_WORDS = 4096
Q_GROUPS_PER_TILE = 2
KV_GROUPS_PER_TILE = WEIGHT_WORDS // BANK
WEIGHT_BUFS = 9
K_LOADS = (8, 8)
V_LOADS = (8, 4, 3, 1)

ROUND_MAGIC = 12582912.0
PI_HI = 3.140625
PI_MID = round((math.pi - PI_HI) * 2.0**27) / 2.0**27
PI_LO = math.pi - PI_HI - PI_MID


def load_groups(nc, w, words, first, count, width, slot):
    nc.sync.dma_start(
        out=w[:, slot * width : (slot + count) * width].rearrange("p (g n) -> p g n", g=count).bitcast(I32),
        in_=words[first : first + count].rearrange("g p n t -> p g (n t)").bitcast(I32),
    )


def load_x(nc, pool, x):
    x_rows = x.rearrange("o s d -> (o s) d")
    chunk_cols = GROUPS_PER_CHUNK * K_PASS
    load_cols = CHUNKS_PER_LOAD * chunk_cols
    chunks = []
    for load in range(X_LOADS):
        x_part = pool.tile([P, load_cols], BF16, name="x_part")
        nc.sync.dma_start(out=x_part[:], in_=x_rows[:, load * load_cols : (load + 1) * load_cols])
        chunks += [x_part[:, c * chunk_cols : (c + 1) * chunk_cols] for c in range(CHUNKS_PER_LOAD)]
    return chunks


def load_scale_block(queue, word, planes, scales, j, quad):
    queue.dma_start(
        out=planes[32 * quad : 32 * quad + PLANES * ROWS, j, :].bitcast(word),
        in_=scales[PLANES * j : PLANES * (j + 1), ROWS * quad : ROWS * (quad + 1), :].bitcast(word),
    )


def quantise_x(nc, stage, psum_t, ident, x_chunks, x_codes, x_scales):
    words_per_group = K_PASS // 2
    groups_per_bank = 2
    for c in range(X_CHUNKS):
        x_words = x_chunks[c].bitcast(F32)
        grouped = stage.tile([P, GROUPS_PER_CHUNK, P, PACK], BF16, align_bytes=64)
        for b in range(GROUPS_PER_CHUNK // groups_per_bank):
            xt = psum_t.tile([P, groups_per_bank, 2, P], F32)
            for gb in range(groups_per_bank):
                first_word = (b * groups_per_bank + gb) * words_per_group
                for u in range(2):
                    nc.tensor.transpose(
                        xt[:, gb, u, :],
                        x_words[:, first_word + u : first_word + words_per_group : 2],
                        ident[:],
                    )
            out_words = grouped[:, b * groups_per_bank : (b + 1) * groups_per_bank, :, :].bitcast(F32)
            in_words = xt[:].rearrange("p g u r -> p g r u")
            if b % 2 == 0:
                nc.vector.tensor_copy(out=out_words, in_=in_words)
            else:
                nc.scalar.copy(out=out_words, in_=in_words)
        groups = slice(c * GROUPS_PER_CHUNK, (c + 1) * GROUPS_PER_CHUNK)
        nc.vector.quantize_mx(
            out=x_codes[:, groups, :].rearrange("p g r -> p (g r)").bitcast(FP8X4),
            scales=x_scales[:, groups, :].rearrange("p g r -> p (g r)"),
            in_=grouped[:].rearrange("p g r t -> p (g r t)"),
        )


def rope_tables(nc, const, position):
    half_angle = const.tile([P, DH], F32)
    nc.vector.tensor_scalar(out=half_angle[:, 0:2], in0=position[:], scalar1=0.5, scalar2=None, op0=ALU.mult)
    for doubling in range(DOUBLINGS):
        width = 2 * 2**doubling
        nc.vector.tensor_scalar(
            out=half_angle[:, width : 2 * width],
            in0=half_angle[:, 0:width],
            scalar1=THETA ** (-width / DH),
            scalar2=None,
            op0=ALU.mult,
        )

    turns = const.tile([P, DH], F32)
    nc.vector.tensor_scalar(
        out=turns[:], in0=half_angle[:], scalar1=1.0 / math.pi, scalar2=ROUND_MAGIC, op0=ALU.mult, op1=ALU.add
    )
    nc.vector.tensor_scalar(out=turns[:], in0=turns[:], scalar1=ROUND_MAGIC, scalar2=None, op0=ALU.subtract)
    reduced = const.tile([P, DH], F32)
    nc.vector.scalar_tensor_tensor(
        out=reduced[:], in0=turns[:], scalar=-PI_HI, in1=half_angle[:], op0=ALU.mult, op1=ALU.add
    )
    for piece in (PI_MID, PI_LO):
        nc.vector.scalar_tensor_tensor(
            out=reduced[:], in0=turns[:], scalar=-piece, in1=reduced[:], op0=ALU.mult, op1=ALU.add
        )

    sin_h = const.tile([P, DH], F32)
    nc.scalar.activation(out=sin_h[:], in_=reduced[:], func=ACT.Sin)
    sin_h2 = const.tile([P, DH], F32)
    nc.scalar.activation(out=sin_h2[:], in_=reduced[:], func=ACT.Sin, scale=0.5)

    cos_h = const.tile([P, DH], F32)
    nc.vector.tensor_mul(out=cos_h[:], in0=sin_h2[:], in1=sin_h2[:])
    nc.vector.tensor_scalar(out=cos_h[:], in0=cos_h[:], scalar1=-2.0, scalar2=1.0, op0=ALU.mult, op1=ALU.add)
    cos_a = const.tile([P, DH], F32)
    nc.vector.tensor_mul(out=cos_a[:], in0=sin_h[:], in1=sin_h[:])
    nc.vector.tensor_scalar(out=cos_a[:], in0=cos_a[:], scalar1=-2.0, scalar2=1.0, op0=ALU.mult, op1=ALU.add)
    sin_a = const.tile([P, DH], F32)
    for cols, sign in ((slice(0, HALF), -1.0), (slice(HALF, DH), 1.0)):
        nc.vector.scalar_tensor_tensor(
            out=sin_a[:, cols], in0=sin_h[:, cols], scalar=2.0 * sign, in1=cos_h[:, cols], op0=ALU.mult, op1=ALU.mult
        )
    return cos_a, sin_a


def rotate(nc, work, results, acc, cos_a, sin_a):
    rotated = results.tile([P, HEADS_PER_BANK, DH], F32)
    nc.vector.tensor_tensor(
        out=rotated[:],
        in0=acc[:].rearrange("p (h i) -> p h i", i=DH),
        in1=cos_a[:].unsqueeze(1).to_broadcast([P, HEADS_PER_BANK, DH]),
        op=ALU.mult,
    )
    halves = acc[:].rearrange("p (h s j) -> p h s j", s=2, j=HALF)
    crossed = work.tile([P, HEADS_PER_BANK, 2, HALF], F32)
    for s in range(2):
        nc.vector.tensor_tensor(
            out=crossed[:, :, s, :],
            in0=halves[:, :, 1 - s, :],
            in1=sin_a[:, s * HALF : (s + 1) * HALF].unsqueeze(1).to_broadcast([P, HEADS_PER_BANK, HALF]),
            op=ALU.mult,
        )
    nc.vector.tensor_add(out=rotated[:], in0=rotated[:], in1=crossed[:].rearrange("p h s j -> p h (s j)"))
    return rotated


def tile_spikinggroupedslidingattention_pa_k_kernel(
    tc, x, Wq_words, Wq_scales, Wk_words, Wk_scales, Wv_words, Wv_scales, out_0, out_1, out_2
):
    nc = tc.nc
    q_out = out_0.rearrange("o h p i -> p (o h) i")
    k_out = out_1.rearrange("o h p i -> p (o h) i")
    v_out = out_2.rearrange("o h p i -> p (o h) i")

    with ExitStack() as ctx:
        ctx.enter_context(tc.manual_schedule())
        const = ctx.enter_context(tc.tile_pool(name="const", bufs=1))
        keep = ctx.enter_context(tc.tile_pool(name="keep", bufs=1))
        x_pool = ctx.enter_context(tc.tile_pool(name="x_pool", bufs=X_LOADS))
        stage = ctx.enter_context(tc.tile_pool(name="stage", bufs=2))
        weights = ctx.enter_context(tc.tile_pool(name="weights", bufs=WEIGHT_BUFS))
        work = ctx.enter_context(tc.tile_pool(name="work", bufs=2))
        results = ctx.enter_context(tc.tile_pool(name="results", bufs=Q_BANKS + 1))
        psum_t = ctx.enter_context(tc.psum_pool(name="psum_t", bufs=2))
        psum_acc = ctx.enter_context(tc.psum_pool(name="psum_acc", bufs=1))

        x_codes = keep.tile([P, GROUPS, P], U32, align_bytes=64)
        x_scales = keep.tile([P, GROUPS, P], U8, align_bytes=64)
        q_planes = keep.tile([P, GROUPS // PLANES, Q_BANKS * BANK], U8, align_bytes=64)
        k_planes = keep.tile([P, GROUPS // PLANES, BANK], U8, align_bytes=64)
        v_planes = keep.tile([P, GROUPS // PLANES, BANK], U8, align_bytes=64)

        for planes in (q_planes, k_planes, v_planes):
            nc.vector.memset(planes[:].rearrange("p j n -> p (j n)").bitcast(I32), 0)
        ident = const.tile([P, P], F32)
        make_identity(nc, ident[:])
        position = const.tile([P, 2], F32)
        nc.gpsimd.iota(
            position[:], pattern=[[0, 2]], base=0, channel_multiplier=1, allow_small_or_imprecise_dtypes=True
        )

        x_chunks = load_x(nc, x_pool, x)
        blocks = [(j, quad) for j in range(GROUPS // PLANES) for quad in range(QUADRANTS)]
        for planes, scales in ((q_planes, Wq_scales), (v_planes, Wv_scales)):
            for j, quad in blocks:
                load_scale_block(nc.gpsimd, F32, planes, scales, j, quad)

        quantise_x(nc, stage, psum_t, ident, x_chunks, x_codes, x_scales)
        cos_a, sin_a = rope_tables(nc, const, position)

        def multiply(acc, g, w_words, w_plane):
            nc.tensor.matmul_mx(
                out=acc[:],
                lhsT=x_codes[:, g, :].bitcast(FP8X4),
                lhsT_scale=x_scales[:, g, :],
                rhs=w_words.bitcast(FP8X4),
                rhs_scale=w_plane,
                start=(g == 0),
                stop=(g == GROUPS - 1),
            )

        acc_q = [psum_acc.tile([P, BANK], F32, name="acc_q%d" % b) for b in range(Q_BANKS)]
        for first in range(0, GROUPS, Q_GROUPS_PER_TILE):
            w = weights.tile([P, WEIGHT_WORDS], U32, align_bytes=64)
            load_groups(nc, w, Wq_words, first, Q_GROUPS_PER_TILE, Q_BANKS * BANK, 0)
            for i in range(Q_GROUPS_PER_TILE):
                g = first + i
                load_scale_block(nc.sync, I32, k_planes, Wk_scales, *blocks[g])
                for b in range(Q_BANKS):
                    word = (i * Q_BANKS + b) * BANK
                    q_plane = q_planes[ROWS * (g % PLANES) : P, g // PLANES, b * BANK : (b + 1) * BANK]
                    multiply(acc_q[b], g, w[:, word : word + BANK], q_plane)
        q_rotated = [rotate(nc, work, results, acc_q[b], cos_a, sin_a) for b in range(Q_BANKS)]

        def project_kv(acc, words, planes, loads):
            g = 0
            for count in loads:
                slot = g % KV_GROUPS_PER_TILE
                if slot == 0:
                    w = weights.tile([P, WEIGHT_WORDS], U32, align_bytes=64)
                load_groups(nc, w, words, g, count, BANK, slot)
                for i in range(slot, slot + count):
                    j, c = divmod(g, PLANES)
                    multiply(acc, g, w[:, i * BANK : (i + 1) * BANK], planes[ROWS * c : P, j, :])
                    g += 1

        acc_k = psum_acc.tile([P, BANK], F32)
        project_kv(acc_k, Wk_words, k_planes, K_LOADS)
        k_rotated = rotate(nc, work, results, acc_k, cos_a, sin_a)

        acc_v = psum_acc.tile([P, BANK], F32)
        project_kv(acc_v, Wv_words, v_planes, V_LOADS)

        for b in range(Q_BANKS):
            nc.sync.dma_start(out=q_out[:, b * HEADS_PER_BANK : (b + 1) * HEADS_PER_BANK, :], in_=q_rotated[b][:])
        nc.sync.dma_start(out=k_out, in_=k_rotated[:])
        v_heads = work.tile([P, HEADS_PER_BANK, DH], F32)
        nc.vector.tensor_copy(out=v_heads[:].rearrange("p h i -> p (h i)"), in_=acc_v[:])
        nc.sync.dma_start(out=v_out, in_=v_heads[:])
